import numpy as np
import ml_dtypes


def mxq(x, axis, fmt="e4m3"):
    dtype, down = {"e4m3": (ml_dtypes.float8_e4m3fn, 7), "e5m2": (ml_dtypes.float8_e5m2, 14)}[fmt]
    v = np.moveaxis(np.asarray(x, np.float32).astype(ml_dtypes.bfloat16).astype(np.float64), axis, -1)
    blocks = v.reshape(v.shape[:-1] + (-1, 32))
    amax = np.abs(blocks).max(-1, keepdims=True)
    byte = np.maximum(np.where(amax > 0, np.frexp(amax)[1] - 1 + 127, 0) - down, 1)
    scale = np.exp2(byte - 127.0)
    codes = (blocks / scale).astype(np.float32).astype(dtype).astype(np.float64)
    return np.moveaxis((codes * scale).reshape(v.shape), -1, axis)


WIDE = False


def mx_kscale(k):
    if not WIDE:
        return np.ones(k)
    levels = np.array([18, -18])
    if k % 512:
        return np.exp2(np.random.permutation(np.resize(levels, k // 32))).repeat(32)
    a = np.empty((k // 512, 16))
    for p in range(k // 512):
        a[p, :8] = np.random.permutation(np.resize(levels, 8))
        for g in range(8):
            far = levels[np.abs(levels - a[p, g]) >= 10]
            a[p, g + 8] = far[np.random.randint(len(far))]
    return np.exp2(a.ravel()).repeat(32)


BF16 = ml_dtypes.bfloat16


def bf(x):
    return np.asarray(x, np.float32).astype(BF16)


def f64(x):
    return np.asarray(x).astype(np.float64)


J, N, X, H, Y = 2, 1024, 1024, 1024, 512
B1 = 2.0 / np.sqrt(X)
B2 = 2.0 / np.sqrt(H)
GAP = 2.0 ** -11


def uni(*sh):
    return np.random.random_sample(sh)


def sample(mu, e, sig):
    return f64(mu) + f64(e) * f64(sig)


def setup_inputs():
    s = mx_kscale(N)[:, None]
    u = mx_kscale(Y)
    v = mx_kscale(H)
    x0 = bf(np.random.standard_normal((N, X)))
    mu_W1 = bf(B1 * (uni(X, H) - 0.5))
    mu_b1 = bf(0.6 * (uni(1, H) - 0.5))
    mu_W2 = bf(B2 * (uni(H, Y) - 0.5))
    mu_b2 = bf(0.6 * (uni(1, Y) - 0.5))
    sig_W1 = bf(B1 * uni(X, H))
    sig_b1 = bf(0.4 * uni(1, H))
    sig_W2 = bf(B2 * uni(H, Y))
    sig_b2 = bf(0.4 * uni(1, Y))
    e_W1 = bf(np.random.standard_normal((J, X, H)))
    e_b1 = bf(np.random.standard_normal((J, 1, H)))
    e_W2 = bf(np.random.standard_normal((J, H, Y)))
    e_b2 = bf(np.random.standard_normal((J, 1, Y)))
    W1 = sample(mu_W1, e_W1, sig_W1)
    b1 = sample(mu_b1, e_b1, sig_b1)
    xf = f64(x0)
    z1 = xf @ W1 + b1
    while True:
        bad = np.nonzero((np.abs(np.abs(z1) - 1.0) < GAP).any(axis=(0, 2)))[0]
        if bad.size == 0:
            break
        xf[bad] = f64(bf(np.random.standard_normal((bad.size, X))))
        z1[:, bad] = xf[bad] @ W1 + b1
    g = 2.0 * np.random.standard_normal((J, N, Y)) * np.exp2(np.random.randint(-6, 1, (J, N, 1)))
    return {
        "x": bf(xf * s),
        "mu_W1": bf(f64(mu_W1) / v),
        "mu_b1": mu_b1,
        "mu_W2": bf(f64(mu_W2) * v[:, None] / u),
        "mu_b2": mu_b2,
        "sig_W1": bf(f64(sig_W1) / v),
        "sig_b1": sig_b1,
        "sig_W2": bf(f64(sig_W2) * v[:, None] / u),
        "sig_b2": sig_b2,
        "e_W1": e_W1,
        "e_b1": e_b1,
        "e_W2": e_W2,
        "e_b2": e_b2,
        "z1": np.asarray(z1, np.float32),
        "grad_out": bf(g / s * u),
    }


def reference(x, mu_W1, mu_b1, mu_W2, mu_b2, sig_W1, sig_b1, sig_W2, sig_b2, e_W1, e_b1, e_W2, e_b2, z1, grad_out):
    W1 = sample(mu_W1, e_W1, sig_W1)
    W2 = sample(mu_W2, e_W2, sig_W2)
    gq = mxq(f64(grad_out), 2, "e5m2")
    w2q = mxq(W2, 2, "e4m3")
    dh = gq @ w2q.transpose(0, 2, 1)
    dz1 = dh * (np.abs(f64(z1)) < 1.0)
    w1q = mxq(W1, 2, "e4m3")
    dx = (mxq(dz1, 2, "e5m2") @ w1q.transpose(0, 2, 1)).sum(axis=0)
    xq = mxq(f64(x), 0, "e4m3")
    dW1 = xq.T @ mxq(dz1, 1, "e5m2")
    dsig_W1 = (f64(e_W1) * dW1).sum(axis=0)
    return dx, dsig_W1

from contextlib import ExitStack

import concourse.mybir as mybir
from concourse.masks import make_identity

J, N, X, H, Y = 2, 1024, 1024, 1024, 512

F32 = mybir.dt.float32
BF16 = mybir.dt.bfloat16
U32 = mybir.dt.uint32
U8 = mybir.dt.uint8
E4M3 = mybir.dt.float8_e4m3fn_x4
E5M2 = mybir.dt.float8_e5m2_x4
ALU = mybir.AluOpType
ACT = mybir.ActivationFunctionType

FLOPS = J * (2 * N * Y * H + 2 * N * H * X + 2 * N * H * X)
BYTES = 2 * (N * X + 2 * X * H + J * X * H + 2 * H * Y + J * H * Y + J * N * Y) + 4 * (J * N * H + N * X + X * H)

P = 128
T = 4


def tile_gaussian_nn_htanh_v_kernel(
    tc, x, mu_W1, mu_b1, mu_W2, mu_b2, sig_W1, sig_b1, sig_W2, sig_b2, e_W1, e_b1, e_W2, e_b2, z1, grad_out, out_0, out_1
):
    nc = tc.nc

    with ExitStack() as ctx:
        const = ctx.enter_context(tc.tile_pool(name="const", bufs=1))
        raw = ctx.enter_context(tc.tile_pool(name="raw", bufs=2))
        work = ctx.enter_context(tc.tile_pool(name="work", bufs=2))
        codes = ctx.enter_context(tc.tile_pool(name="codes", bufs=1))
        psum = ctx.enter_context(tc.psum_pool(name="psum", bufs=4))

        ident_f = const.tile([P, P], F32, name="ident_f", tag="ident_f")
        make_identity(nc, ident_f[:])
        ident_b = const.tile([P, P], BF16, name="ident_b", tag="ident_b")
        nc.vector.tensor_copy(out=ident_b[:], in_=ident_f[:])

        def copy_to(engine, out, in_):
            if engine == "s":
                nc.scalar.copy(out=out, in_=in_)
            else:
                nc.vector.tensor_copy(out=out, in_=in_)

        def code_tile(name, width, tag, bufs):
            c = codes.tile([P, width], U32, name=name, tag=tag, bufs=bufs, align_bytes=64)
            s = codes.tile([P, width], U8, name=name + "_s", tag=tag + "_s", bufs=bufs, align_bytes=64)
            return c, s

        def quantize(dst, c0, c1, fmt, src):
            nc.vector.quantize_mx(out=dst[0][:, c0:c1].bitcast(fmt), scales=dst[1][:, c0:c1], in_=src)

        def grp_tile(name):
            return work.tile([P, 512, T], BF16, name=name, tag="grp", bufs=6, align_bytes=64)

        def load_w2_const(q):
            v = sig_W2.rearrange("(q b m) y -> q m b y", q=2, b=4)
            sg = raw.tile([P, 4, Y], BF16, name="sg2", tag="w2s", bufs=4)
            nc.sync.dma_start(out=sg[:], in_=v[q])
            v = mu_W2.rearrange("(q b m) y -> q m b y", q=2, b=4)
            mu = raw.tile([P, 4, Y], BF16, name="mu2", tag="w2s", bufs=4)
            nc.sync.dma_start(out=mu[:], in_=v[q])
            return sg, mu

        def load_e2(j, q):
            v = e_W2[j].rearrange("(q b m) y -> q m b y", q=2, b=4)
            e = raw.tile([P, 4, Y], BF16, name="e2", tag="in4", bufs=4)
            nc.sync.dma_start(out=e[:], in_=v[q])
            return e

        def load_grad(j, g):
            v = grad_out[j].rearrange("(g p t) y -> g p t y", g=2, t=T)
            t = raw.tile([P, T, Y], BF16, name="gr", tag="in4", bufs=4)
            nc.sync.dma_start(out=t[:], in_=v[g])
            return t

        def load_x(g, half):
            v = x.rearrange("(g p t) w -> g p t w", g=2, t=T)
            t = raw.tile([P, T, 512], BF16, name="xr", tag="in4", bufs=4)
            nc.sync.dma_start(out=t[:], in_=v[g][:, :, 512 * half : 512 * half + 512])
            return t

        def load_z(j, g, t):
            v = z1[j].rearrange("(g p t) h -> g t p h", g=2, t=T)
            zt = raw.tile([P, H], F32, name="z", tag="z", bufs=4)
            nc.sync.dma_start(out=zt[:], in_=v[g, t])
            return zt

        def load_w1(i):
            rows = slice(P * i, P * i + P)
            sg = raw.tile([P, H], BF16, name="sg1", tag="sg1", bufs=3)
            nc.sync.dma_start(out=sg[:], in_=sig_W1[rows, :])
            es = []
            for j in range(J):
                e = raw.tile([P, H], BF16, name="e1", tag="e1", bufs=16)
                nc.sync.dma_start(out=e[:], in_=e_W1[j][rows, :])
                es.append(e)
            mu = raw.tile([P, H], BF16, name="mu1", tag="mu1", bufs=3)
            nc.sync.dma_start(out=mu[:], in_=mu_W1[rows, :])
            return sg, es, mu

        def multiply(engine, e, sg):
            prod = work.tile([P, 2, T, P], F32, name="prod", tag="prod", bufs=3)
            eng = nc.gpsimd if engine == "g" else nc.vector
            eng.tensor_tensor(
                out=prod[:],
                in0=e.rearrange("p b (w t) -> p b t w", t=T),
                in1=sg.rearrange("p b (w t) -> p b t w", t=T),
                op=ALU.mult,
            )
            return prod

        def turn(prod_b, mu_b, out, engine):
            bank = psum.tile([P, T, P], F32, name="tp", tag="tp", bufs=4)
            for t in range(T):
                nc.tensor.matmul(bank[:, t, :], lhsT=prod_b[:, t, :], rhs=ident_f[:], is_transpose=True, start=(t == 0), stop=False)
            for t in range(T):
                nc.tensor.matmul(bank[:, t, :], lhsT=mu_b[:, t::T], rhs=ident_b[:], start=False, stop=(t == T - 1))
            copy_to(engine, out, bank[:].rearrange("w t r -> w r t"))

        def turn_words(words, grp, t_pair, engine):
            bank = psum.tile([P, 2, 2, P], F32, name="tp", tag="tp", bufs=4)
            for a in range(2):
                for u in range(2):
                    nc.tensor.transpose(bank[:, a, u, :], words[:, a, u::2], ident_f[:])
            out = grp[:, 256 * t_pair : 256 * t_pair + 256, :].rearrange("p c k -> p (c k)").bitcast(F32)
            copy_to(engine, out.rearrange("p (a m u) -> p a m u", a=2, u=2), bank[:].rearrange("p a u m -> p a m u"))

        w2c = {}
        gc = {}
        xc = []
        w1c = {}
        dzc = {}
        dzt = {}

        w2_const = {}

        def build_w2(j, q, e, mult_engine="v", copy_engine="s"):
            sg, mu = w2_const[q]
            grp = grp_tile("w2g")
            for r in range(2):
                prod = multiply(mult_engine, e[:, 2 * r : 2 * r + 2, :], sg[:, 2 * r : 2 * r + 2, :])
                for b in range(2):
                    c0 = P * (2 * r + b)
                    turn(prod[:, b], mu[:, 2 * r + b, :], grp[:, c0 : c0 + P, :], copy_engine)
            c = code_tile("w2c", 512, "w2c", 3)
            quantize(c, 0, 512, E4M3, grp[:].rearrange("p c k -> p (c k)"))
            w2c[j, q] = c

        def build_grad(j, g, gr, copy_engine="s"):
            grp = grp_tile("gg")
            words = gr[:].rearrange("p t y -> p (t y)").bitcast(F32).rearrange("p (t w) -> p t w", t=T)
            for tp in range(2):
                turn_words(words[:, 2 * tp : 2 * tp + 2, :], grp, tp, copy_engine)
            c = code_tile("gc", 512, "gc", 3)
            quantize(c, 0, 512, E5M2, grp[:].rearrange("p c k -> p (c k)"))
            gc[j, g] = c

        def build_x(g, half, xr, engine="v"):
            if half == 0:
                xc.append(code_tile("xc%d" % g, X, "xc%d" % g, 1))
            grp = grp_tile("xg")
            if engine == "g":
                nc.gpsimd.tensor_scalar(out=grp[:], in0=xr[:].rearrange("p t w -> p w t"), scalar1=1.0, scalar2=0.0, op0=ALU.mult, op1=ALU.add)
            else:
                copy_to(engine, grp[:], xr[:].rearrange("p t w -> p w t"))
            quantize(xc[g], 512 * half, 512 * half + 512, E4M3, grp[:].rearrange("p c k -> p (c k)"))

        w1g = {}

        def w1_steps(i, j, sg, es, mu, mult_engine, copy_engine="s"):
            made = {}

            def first():
                if i == 0:
                    for c in range(2):
                        w1c[j, c] = code_tile("w1c%d%d" % (j, c), X, "w1c%d%d" % (j, c), 1)
                made["prod"] = multiply(
                    mult_engine, es[j][:].rearrange("p (b y) -> p b y", b=2), sg[:].rearrange("p (b y) -> p b y", b=2)
                )

            def second():
                for c in range(2):
                    if i % 4 == 0:
                        w1g[j, c] = grp_tile("w1g")
                    c0 = P * (i % 4)
                    turn(made["prod"][:, c], mu[:, 512 * c : 512 * c + 512], w1g[j, c][:, c0 : c0 + P, :], copy_engine)

            def third():
                for c in range(2):
                    h0 = 512 * (i // 4)
                    quantize(w1c[j, c], h0, h0 + 512, E4M3, w1g[j, c][:].rearrange("p c k -> p (c k)"))

            return [first, second] + ([third] if i % 4 == 3 else [])

        def dz_steps(j, g, zs, inter_engines="ss", copy_engine="s"):
            dz = {}
            grp = {}

            def absolute(t):
                nc.scalar.activation(out=zs[t][:], in_=zs[t][:], func=ACT.Abs)

            def mask(t):
                for q in range(2):
                    if t == 0:
                        dz[q] = work.tile([P, T, 512], BF16, name="dz", tag="dz", bufs=4, align_bytes=64)
                    bank = psum.tile([P, 512], F32, name="mm", tag="mm", bufs=4)
                    nc.tensor.matmul_mx(
                        out=bank[:],
                        lhsT=gc[j, g][0][:, P * t : P * t + P].bitcast(E5M2),
                        lhsT_scale=gc[j, g][1][:, P * t : P * t + P],
                        rhs=w2c[j, q][0][:].bitcast(E4M3),
                        rhs_scale=w2c[j, q][1][:],
                        start=True,
                        stop=True,
                    )
                    nc.vector.scalar_tensor_tensor(
                        out=dz[q][:, t, :], in0=zs[t][:, 512 * q : 512 * q + 512], scalar=1.0, in1=bank[:], op0=ALU.is_lt, op1=ALU.mult
                    )

            def turn_pair(q, half):
                if half == 0:
                    grp[q] = grp_tile("dg")
                words = dz[q][:].rearrange("p t y -> p (t y)").bitcast(F32).rearrange("p (t w) -> p t w", t=T)
                turn_words(words[:, 2 * half : 2 * half + 2, :], grp[q], half, copy_engine)

            def interleave(q):
                if q == 0:
                    dzc[j, g] = code_tile("dzc%d%d" % (j, g), H, "dzc%d%d" % (j, g), 1)
                    dzt[j, g] = code_tile("dzt%d%d" % (j, g), H, "dzt%d%d" % (j, g), 1)
                inter = grp_tile("di")
                grp[2 + q] = inter
                copy_to(inter_engines[q], inter[:], dz[q][:].rearrange("p t h -> p h t"))

            def quant(q):
                quantize(dzt[j, g], 512 * q, 512 * q + 512, E5M2, grp[q][:].rearrange("p c k -> p (c k)"))

            def quant2(q):
                quantize(dzc[j, g], 512 * q, 512 * q + 512, E5M2, grp[2 + q][:].rearrange("p c k -> p (c k)"))

            return [
                lambda: absolute(0),
                lambda: absolute(1),
                lambda: mask(0),
                lambda: (absolute(2), mask(1)),
                lambda: (turn_pair(0, 0), absolute(3), mask(2)),
                lambda: turn_pair(1, 0),
                lambda: mask(3),
                lambda: turn_pair(0, 1),
                lambda: interleave(0),
                lambda: turn_pair(1, 1),
                lambda: quant(0),
                lambda: interleave(1),
                lambda: (quant(1), quant2(0)),
                lambda: quant2(1),
            ]

        def dx(g, t, copy_engine="s"):
            ot = raw.tile([P, X], F32, name="ot", tag="in4", bufs=4)
            for xh in range(2):
                bank = psum.tile([P, 512], F32, name="mm", tag="mm", bufs=4)
                for k in range(4):
                    j, c = divmod(k, 2)
                    cols = slice(512 * c + P * t, 512 * c + P * t + P)
                    xcols = slice(512 * xh, 512 * xh + 512)
                    nc.tensor.matmul_mx(
                        out=bank[:],
                        lhsT=dzt[j, g][0][:, cols].bitcast(E5M2),
                        lhsT_scale=dzt[j, g][1][:, cols],
                        rhs=w1c[j, c][0][:, xcols].bitcast(E4M3),
                        rhs_scale=w1c[j, c][1][:, xcols],
                        start=(k == 0),
                        stop=(k == 3),
                    )
                copy_to(copy_engine, ot[:, 512 * xh : 512 * xh + 512], bank[:])
            nc.sync.dma_start(out=out_0.rearrange("(g m t) x -> g t m x", g=2, t=T)[g, t], in_=ot[:])

        def dw(i, es, add_engine="v"):
            parts = []
            for j in range(J):
                part = raw.tile([P, H], F32, name="part", tag="w2s", bufs=4)
                for hh in range(2):
                    hc = slice(512 * hh, 512 * hh + 512)
                    bank = psum.tile([P, 512], F32, name="mm", tag="mm", bufs=4)
                    for g in range(2):
                        nc.tensor.matmul_mx(
                            out=bank[:],
                            lhsT=xc[g][0][:, P * i : P * i + P].bitcast(E4M3),
                            lhsT_scale=xc[g][1][:, P * i : P * i + P],
                            rhs=dzc[j, g][0][:, hc].bitcast(E5M2),
                            rhs_scale=dzc[j, g][1][:, hc],
                            start=(g == 0),
                            stop=(g == 1),
                        )
                    nc.vector.tensor_tensor(out=part[:, hc], in0=es[j][:, hc], in1=bank[:], op=ALU.mult)
                parts.append(part)
            eng = nc.gpsimd if add_engine == "g" else nc.vector
            eng.tensor_tensor(out=parts[0][:], in0=parts[0][:], in1=parts[1][:], op=ALU.add)
            nc.sync.dma_start(out=out_1[P * i : P * i + P, :], in_=parts[0][:])

        def run(*lists):
            order = []
            for k in range(len(lists)):
                n = len(lists[k])
                for i in range(n):
                    order.append(((i + 0.5) / n, k, i))
            for at, k, i in sorted(order):
                lists[k][i]()

        e2 = {}
        gr = {}
        for q in range(2):
            sg = raw.tile([P, 4, Y], BF16, name="sg2", tag="w2s", bufs=4)
            nc.sync.dma_start(out=sg[:], in_=sig_W2.rearrange("(q b m) y -> q m b y", q=2, b=4)[q])
            e2[0, q] = load_e2(0, q)
            mu = raw.tile([P, 4, Y], BF16, name="mu2", tag="w2s", bufs=4)
            nc.sync.dma_start(out=mu[:], in_=mu_W2.rearrange("(q b m) y -> q m b y", q=2, b=4)[q])
            w2_const[q] = (sg, mu)
            gr[0, q] = load_grad(0, q)
        z00 = [load_z(0, 0, t) for t in range(T)]
        w1 = {}
        w1[0] = load_w1(0)
        build_w2(0, 0, e2[0, 0])
        build_grad(0, 0, gr[0, 0])
        build_w2(0, 1, e2[0, 1])
        build_grad(0, 1, gr[0, 1])
        w1[1] = load_w1(1)

        def w1_list(items, engines):
            res = []
            for i in items:
                for j in range(J):
                    res += w1_steps(i, j, w1[i][0], w1[i][1], w1[i][2], engines[j])
            return res

        w1[2] = load_w1(2)
        z01 = [load_z(0, 1, t) for t in range(T)]
        run(dz_steps(0, 0, z00, "vs"), w1_list([0, 1, 2], "vg"))
        for i in range(3, 6):
            w1[i] = load_w1(i)
        for q in range(2):
            e2[1, q] = load_e2(1, q)
            gr[1, q] = load_grad(1, q)
        run(dz_steps(0, 1, z01, "vs"), w1_list([3, 4, 5], "vg"))
        z10 = [load_z(1, 0, t) for t in range(T)]
        for i in range(6, 8):
            w1[i] = load_w1(i)
        for q in range(2):
            build_w2(1, q, e2[1, q])
            build_grad(1, q, gr[1, q])
        xr = [load_x(0, 0), load_x(0, 1), load_x(1, 0), load_x(1, 1)]
        run(dz_steps(1, 0, z10, "vs"), w1_list([6, 7], "vv"), [lambda: build_x(0, 0, xr[0], "g"), lambda: build_x(0, 1, xr[1], "g")])
        z11 = [load_z(1, 1, t) for t in range(T)]
        run(
            dz_steps(1, 1, z11, "vs"),
            [lambda: dx(0, 0), lambda: dx(0, 1), lambda: dx(0, 2), lambda: dx(0, 3)],
            [lambda: build_x(1, 0, xr[2], "g"), lambda: build_x(1, 1, xr[3], "g")],
        )
        for i in range(8):
            dw(i, w1[i][1], "g" if i % 2 == 0 and i < 7 else "v")
            if i % 2 == 1:
                dx(1, i // 2)
